import numpy as np
import ml_dtypes


def mxq(x, axis, fmt="e4m3"):
    dtype, down = {"e4m3": (ml_dtypes.float8_e4m3fn, 7), "e5m2": (ml_dtypes.float8_e5m2, 14)}[fmt]
    v = np.moveaxis(np.asarray(x, np.float32).astype(ml_dtypes.bfloat16).astype(np.float64), axis, -1)
    blocks = v.reshape(v.shape[:-1] + (-1, 32))
    amax = np.abs(blocks).max(-1, keepdims=True)
    byte = np.maximum(np.where(amax > 0, np.frexp(amax)[1] - 1 + 127, 0) - down, 1)
    scale = np.exp2(byte - 127.0)
    codes = (blocks / scale).astype(np.float32).astype(dtype).astype(np.float64)
    return np.moveaxis((codes * scale).reshape(v.shape), -1, axis)


WIDE = False


def mx_kscale(k):
    if not WIDE:
        return np.ones(k)
    levels = np.array([20, -20, 10, -10, 0])
    a = np.random.permutation(np.resize(levels, k // 512 * 4)).reshape(k // 512, 4)
    idx = np.arange(k)
    return np.exp2(a[idx // 512, idx % 128 // 32])


BF16 = ml_dtypes.bfloat16


def bf(x):
    return np.asarray(x, np.float32).astype(BF16)


def f64(x):
    return np.asarray(x).astype(np.float64)


B, H, Wd, C_IN, KH, KW, OUT = 4, 16, 32, 456, 3, 3, 513
N = KH * KW
HCAT = (C_IN - 1) * N + 1
T = B * H * Wd
CURV = 1.0
SIG = 0.1004
HN = np.sqrt(1.0 / CURV + 2.0 * (HCAT - 1) * SIG ** 2)
GS = 0.5


def hcat(x):
    Bn, Hn, Wn, C = x.shape
    xp = np.pad(x, ((0, 0), (1, 1), (1, 1), (0, 0)), mode="edge")
    slabs = [xp[:, i:i + Hn, j:j + Wn, :] for i in range(KH) for j in range(KW)]
    patches = np.stack(slabs, axis=3)
    t_cat = np.sqrt(np.sum(patches[..., 0] ** 2, axis=-1) - (N - 1) / CURV)
    sp = patches[..., 1:].reshape(Bn, Hn, Wn, N * (C - 1))
    return np.concatenate([t_cat[..., None], sp], axis=-1).reshape(Bn * Hn * Wn, N * (C - 1) + 1)


def image_scale():
    k = mx_kscale(T)
    lv = np.unique(np.concatenate([np.ones(1), np.maximum(k, 1.0 / k)]))
    return lv[(np.arange(B) * len(lv)) // B]


def setup_inputs():
    si = image_scale()[:, None, None, None]
    v = np.random.standard_normal((B, H, Wd, C_IN - 1)) * SIG
    t = np.sqrt(1.0 / CURV + np.sum(v * v, axis=-1, keepdims=True))
    x0 = bf(np.concatenate([t, v], axis=-1))
    W = bf(np.random.standard_normal((OUT - 1, HCAT)) * (4.8 / (HN * np.sqrt(OUT - 1))))
    b = bf(np.random.standard_normal(OUT - 1) * (1.4 / np.sqrt(OUT - 1)))
    g = bf(np.random.standard_normal((B, H, Wd, OUT)) * np.exp2(np.random.randint(-12, 1, (B, H, Wd, 1))) * GS / si)
    z = (hcat(f64(x0)) @ f64(W).T + f64(b)).reshape(B, H, Wd, OUT - 1)
    t0 = f64(x0)[..., :1]
    tw = np.sqrt(si ** 2 * t0 ** 2 - (N - 1) / (N * CURV) * (si ** 2 - 1.0))
    x = bf(np.concatenate([tw, f64(x0)[..., 1:] * si], axis=-1))
    return {"x": x, "W": W, "b": b, "z": np.asarray(z, np.float32), "grad_out": g}


def reference(x, W, b, z, grad_out):
    h = hcat(f64(x))
    zf = f64(z).reshape(T, OUT - 1)
    g = f64(grad_out).reshape(T, OUT)
    t_out = np.sqrt(1.0 / CURV + np.sum(zf * zf, axis=1, keepdims=True))
    dz = g[:, 1:] + g[:, :1] * zf / t_out
    return mxq(dz, 0, "e5m2").T @ mxq(h, 0, "e4m3")

@@ -1,0 +1,238 @@
+from contextlib import ExitStack
+
+import concourse.mybir as mybir
+
+FLOPS = 2 * 2048 * 512 * 4096
+BYTES = 2 * 2048 * 456 + 4 * 2048 * 512 + 2 * 2048 * 513 + 4 * 512 * 4096
+
+F32 = mybir.dt.float32
+BF16 = mybir.dt.bfloat16
+U32 = mybir.dt.uint32
+U8 = mybir.dt.uint8
+E4M3_X4 = mybir.dt.float8_e4m3fn_x4
+E5M2_X4 = mybir.dt.float8_e5m2_x4
+ACT = mybir.ActivationFunctionType
+ALU = mybir.AluOpType
+
+P = 128
+PACK = 4
+ROW_PARTS = 8
+IMAGES = 4
+IMAGE_PARTS = 32
+PASSES = 4
+TOP = 0
+BOTTOM = PASSES + 1
+ROW_TILES = PASSES + 2
+SLOTS = PACK + 2
+C_IN = 456
+C_PAD = 464
+SPACE = C_IN - 1
+G_IN = 513
+G_PAD = 2064
+M_ALL = 512
+M_TILE = 128
+M_TILES = M_ALL // M_TILE
+N_TILE = 512
+H_COLS = 4096
+STORE_ALIGN = 8
+RUN = 4
+
+FIRST_TAPS = [(1, 1), (2, 1)]
+LATER_TAPS = [(0, 1), (1, 0), (2, 0), (1, 2), (2, 2), (0, 2), (0, 0)]
+T_CAT_TAP = (1, 2)
+GROUPED_BUFS = 4
+
+
+def regrouped(rows, grouped):
+    return (
+        rows.rearrange("p t (c i) -> p c t i", i=RUN),
+        grouped.rearrange("p (c i) t -> p c t i", i=RUN),
+    )
+
+
+def tile_hypconvhyperboloid_v_kernel(tc, x, W, b, z, grad_out, out):
+    nc = tc.nc
+
+    z_tiles = z.rearrange("b (rh a) (pp t) m -> a (b rh) pp (t m)", a=PASSES, t=PACK)
+    g_tiles = grad_out.rearrange("b (rh a) (pp t) m -> a (b rh) pp (t m)", a=PASSES, t=PACK)
+    x_tiles = x.rearrange("b (rh a) (pp t) c -> a (b rh) pp (t c)", a=PASSES, t=PACK)
+    x_pixels = x.rearrange("b (rh a) q c -> q (b rh) a c", a=PASSES)
+
+    with ExitStack() as stack:
+        keep = stack.enter_context(tc.tile_pool(name="keep", bufs=1))
+        small = stack.enter_context(tc.tile_pool(name="small", bufs=1))
+        psum = stack.enter_context(tc.psum_pool(name="psum", bufs=8))
+
+        x_win = keep.tile([P, ROW_TILES, SLOTS, C_PAD], BF16)
+        x_codes = keep.tile([P, ROW_TILES, 3, N_TILE], U32, align_bytes=64)
+        x_scales = keep.tile([P, ROW_TILES, 3, N_TILE], U8, align_bytes=64)
+        dz_codes = keep.tile([P, PASSES, M_ALL], U32, align_bytes=64)
+        dz_scales = keep.tile([P, PASSES, M_ALL], U8, align_bytes=64)
+        grouped_bufs = [
+            keep.tile([P, N_TILE, PACK], BF16, align_bytes=64, name="grouped%d" % k)
+            for k in range(GROUPED_BUFS)
+        ]
+        for grouped in grouped_bufs:
+            nc.vector.memset(grouped[:, C_IN:N_TILE, :], 0.0)
+
+        one = small.tile([P, 1], F32)
+        nc.vector.memset(one[:], 1.0)
+        nc.scalar.activation(out=one[:], in_=one[:], func=ACT.Sqrt)
+
+        t_cat = small.tile([P, PASSES, PACK], BF16)
+        made = []
+
+        def quantise_x(u, j, copy):
+            if (u, j) in made:
+                return
+            grouped = grouped_bufs[len(made) % GROUPED_BUFS]
+            made.append((u, j))
+            src, dst = regrouped(x_win[:, u, j : j + PACK, 0:C_IN], grouped[:, 0:C_IN, :])
+            copy(out=dst, in_=src)
+            if j == T_CAT_TAP[1] and TOP < u < BOTTOM:
+                nc.vector.tensor_copy(out=grouped[:, 0, :], in_=t_cat[:, u - 1, :])
+            nc.vector.quantize_mx(
+                out=x_codes[:, u, j, :].bitcast(E4M3_X4),
+                scales=x_scales[:, u, j, :],
+                in_=grouped[:].rearrange("p c t -> p (c t)"),
+            )
+
+        def multiply(acc, tap, m, a, start, stop):
+            i, j = tap
+            m_cols = slice(m * M_TILE, (m + 1) * M_TILE)
+            nc.tensor.matmul_mx(
+                out=acc[:],
+                lhsT=dz_codes[:, a, m_cols].bitcast(E5M2_X4),
+                lhsT_scale=dz_scales[:, a, m_cols],
+                rhs=x_codes[:, a + i, j, :].bitcast(E4M3_X4),
+                rhs_scale=x_scales[:, a + i, j, :],
+                start=start,
+                stop=stop,
+            )
+
+        def fill_edge_tiles(slots):
+            nc.sync.dma_start(
+                out=x_win[ROW_PARTS:P, TOP, slots, 0:C_IN], in_=x_win[0 : P - ROW_PARTS, PASSES, slots, 0:C_IN]
+            )
+            nc.sync.dma_start(
+                out=x_win[0 : P - ROW_PARTS, BOTTOM, slots, 0:C_IN], in_=x_win[ROW_PARTS:P, 1, slots, 0:C_IN]
+            )
+            for image in range(IMAGES):
+                first = slice(image * IMAGE_PARTS, image * IMAGE_PARTS + ROW_PARTS)
+                last = slice((image + 1) * IMAGE_PARTS - ROW_PARTS, (image + 1) * IMAGE_PARTS)
+                nc.sync.dma_start(out=x_win[first, TOP, slots, 0:C_IN], in_=x_win[first, 1, slots, 0:C_IN])
+                nc.sync.dma_start(out=x_win[last, BOTTOM, slots, 0:C_IN], in_=x_win[last, PASSES, slots, 0:C_IN])
+
+        first_acc = {}
+        for tap in FIRST_TAPS:
+            for m in range(M_TILES):
+                first_acc[(tap, m)] = psum.tile(
+                    [M_TILE, N_TILE], F32, name="acc_first_%d_%d" % (tap[0], m), tag="acc"
+                )
+
+        with tc.tile_pool(name="dz_work", bufs=2) as work, tc.tile_pool(name="dz_in", bufs=1) as dz_in:
+            z_sb = dz_in.tile([P, PASSES, PACK, M_ALL], F32)
+            g_sb = dz_in.tile([P, PASSES, G_PAD], BF16)
+
+            loaded = []
+            for a in range(PASSES):
+                nc.sync.dma_start(out=z_sb[:, a].rearrange("p t m -> p (t m)"), in_=z_tiles[a])
+                nc.sync.dma_start(out=g_sb[:, a, 0 : PACK * G_IN], in_=g_tiles[a])
+                for i, j in FIRST_TAPS:
+                    u = a + i
+                    if u < BOTTOM and u not in loaded:
+                        loaded.append(u)
+                        nc.sync.dma_start(out=x_win[:, u, 1 : 1 + PACK, 0:C_IN], in_=x_tiles[u - 1])
+            fill_edge_tiles(slice(1, 1 + PACK))
+            for pp in range(ROW_PARTS):
+                nc.sync.dma_start(
+                    out=x_win[pp:P:ROW_PARTS, 1 : 1 + PASSES, 0, 0:C_IN],
+                    in_=x_pixels[max(PACK * pp - 1, 0)],
+                )
+                nc.sync.dma_start(
+                    out=x_win[pp:P:ROW_PARTS, 1 : 1 + PASSES, SLOTS - 1, 0:C_IN],
+                    in_=x_pixels[min(PACK * pp + PACK, 31)],
+                )
+            fill_edge_tiles(slice(0, SLOTS, SLOTS - 1))
+
+            for a in range(PASSES):
+                g_tokens = g_sb[:, a, 0 : PACK * G_IN].rearrange("p (t m) -> p t m", t=PACK)
+                squares = work.tile([P, PACK, M_ALL], BF16)
+                sum_sq = work.tile([P, PACK], F32)
+                for t in range(PACK):
+                    nc.scalar.activation(
+                        out=squares[:, t, :], in_=z_sb[:, a, t, :], func=ACT.Square,
+                        accum_out=sum_sq[:, t : t + 1],
+                    )
+                t_out = work.tile([P, PACK], F32)
+                nc.scalar.activation(out=t_out[:], in_=sum_sq[:], func=ACT.Sqrt, bias=1.0)
+                inv_t_out = work.tile([P, PACK], F32)
+                nc.vector.reciprocal(out=inv_t_out[:], in_=t_out[:])
+                slope = work.tile([P, PACK], F32)
+                nc.vector.tensor_tensor(out=slope[:], in0=g_tokens[:, :, 0], in1=inv_t_out[:], op=ALU.mult)
+                dz_rows = work.tile([P, PACK, M_ALL], BF16)
+                for t in range(PACK):
+                    nc.vector.scalar_tensor_tensor(
+                        out=dz_rows[:, t, :], in0=z_sb[:, a, t, :], scalar=slope[:, t : t + 1],
+                        in1=g_tokens[:, t, 1:G_IN], op0=ALU.mult, op1=ALU.add,
+                    )
+                dz_grouped = work.tile([P, M_ALL, PACK], BF16, align_bytes=64)
+                src, dst = regrouped(dz_rows[:], dz_grouped[:])
+                nc.vector.tensor_copy(out=dst, in_=src)
+                nc.vector.quantize_mx(
+                    out=dz_codes[:, a, :].bitcast(E5M2_X4),
+                    scales=dz_scales[:, a, :],
+                    in_=dz_grouped[:].rearrange("p m t -> p (m t)"),
+                )
+                for i, j in FIRST_TAPS:
+                    quantise_x(a + i, j, nc.scalar.copy)
+                for m in range(M_TILES):
+                    for tap in FIRST_TAPS:
+                        multiply(first_acc[(tap, m)], tap, m, a, a == 0, a == PASSES - 1)
+
+        time_sq = small.tile([P, ROW_TILES, SLOTS], F32)
+        nc.vector.tensor_tensor(out=time_sq[:], in0=x_win[:, :, :, 0], in1=x_win[:, :, :, 0], op=ALU.mult)
+        pair_q = small.tile([P, ROW_TILES, PACK], F32)
+        nc.vector.tensor_tensor(out=pair_q[:], in0=time_sq[:, :, 0:PACK], in1=time_sq[:, :, 1 : 1 + PACK], op=ALU.add)
+        sum_q = small.tile([P, ROW_TILES, PACK], F32)
+        nc.vector.tensor_tensor(out=sum_q[:], in0=pair_q[:], in1=time_sq[:, :, 2 : 2 + PACK], op=ALU.add)
+        pair_r = small.tile([P, PASSES, PACK], F32)
+        nc.vector.tensor_tensor(out=pair_r[:], in0=sum_q[:, 0:PASSES, :], in1=sum_q[:, 1 : 1 + PASSES, :], op=ALU.add)
+        sum_taps = small.tile([P, PASSES, PACK], F32)
+        nc.vector.tensor_tensor(out=sum_taps[:], in0=pair_r[:], in1=sum_q[:, 2 : 2 + PASSES, :], op=ALU.add)
+        nc.scalar.activation(out=t_cat[:], in_=sum_taps[:], func=ACT.Sqrt, bias=-8.0)
+
+        for i, j in LATER_TAPS:
+            for a in range(PASSES):
+                quantise_x(a + i, j, nc.vector.tensor_copy)
+
+        rows_pool = stack.enter_context(tc.tile_pool(name="rows", bufs=1))
+        out_rows = [rows_pool.tile([M_TILE, H_COLS], F32, name="out_rows%d" % m) for m in range(M_TILES)]
+        stored = []
+
+        def empty_and_store(acc, tap, m):
+            n = 3 * tap[0] + tap[1]
+            first = 1 + SPACE * n
+            last = first + SPACE
+            nc.scalar.copy(out=out_rows[m][:, first:last], in_=acc[:, 1:C_IN])
+            if tap == T_CAT_TAP:
+                nc.scalar.copy(out=out_rows[m][:, 0:1], in_=acc[:, 0:1])
+            left_there = (n - 1 in stored) if n > 0 else (3 * T_CAT_TAP[0] + T_CAT_TAP[1] in stored)
+            right_there = n + 1 in stored
+            lo = first - first % STORE_ALIGN if left_there else first + (-first) % STORE_ALIGN
+            hi = last + (-last) % STORE_ALIGN if right_there else last - last % STORE_ALIGN
+            nc.sync.dma_start(out=out[m * M_TILE : (m + 1) * M_TILE, lo:hi], in_=out_rows[m][:, lo:hi])
+
+        for tap in FIRST_TAPS:
+            for m in range(M_TILES):
+                empty_and_store(first_acc[(tap, m)], tap, m)
+            stored.append(3 * tap[0] + tap[1])
+        for tap in LATER_TAPS:
+            accs = [psum.tile([M_TILE, N_TILE], F32, name="acc%d" % m, tag="acc") for m in range(M_TILES)]
+            passes = sorted(range(PASSES), key=lambda a: made.index((a + tap[0], tap[1])))
+            for a in passes:
+                for m in range(M_TILES):
+                    multiply(accs[m], tap, m, a, a == passes[0], a == passes[-1])
+            for m in range(M_TILES):
+                empty_and_store(accs[m], tap, m)
+            stored.append(3 * tap[0] + tap[1])

@@ -35,7 +35,6 @@ M_TILES = M_ALL // M_TILE
 N_TILE = 512
 H_COLS = 4096
 STORE_ALIGN = 8
-RUN = 4
 
 FIRST_TAPS = [(1, 1), (2, 1)]
 LATER_TAPS = [(0, 1), (1, 0), (2, 0), (1, 2), (2, 2), (0, 2), (0, 0)]
@@ -44,10 +43,7 @@ GROUPED_BUFS = 4
 
 
 def regrouped(rows, grouped):
-    return (
-        rows.rearrange("p t (c i) -> p c t i", i=RUN),
-        grouped.rearrange("p (c i) t -> p c t i", i=RUN),
-    )
+    return rows.rearrange("p t c -> p c t"), grouped
 
 
 def tile_hypconvhyperboloid_v_kernel(tc, x, W, b, z, grad_out, out):

@@ -226,9 +226,8 @@ def tile_hypconvhyperboloid_v_kernel(tc, x, W, b, z, grad_out, out):
         for tap in LATER_TAPS:
             accs = [psum.tile([M_TILE, N_TILE], F32, name="acc%d" % m, tag="acc") for m in range(M_TILES)]
             passes = sorted(range(PASSES), key=lambda a: made.index((a + tap[0], tap[1])))
-            for a in passes:
-                for m in range(M_TILES):
-                    multiply(accs[m], tap, m, a, a == passes[0], a == passes[-1])
             for m in range(M_TILES):
+                for a in passes:
+                    multiply(accs[m], tap, m, a, a == passes[0], a == passes[-1])
                 empty_and_store(accs[m], tap, m)
             stored.append(3 * tap[0] + tap[1])

@@ -40,6 +40,7 @@ FIRST_TAPS = [(1, 1), (2, 1)]
 LATER_TAPS = [(0, 1), (1, 0), (2, 0), (1, 2), (2, 2), (0, 2), (0, 0)]
 T_CAT_TAP = (1, 2)
 GROUPED_BUFS = 4
+M_HALF = M_ALL // 2
 
 
 def regrouped(rows, grouped):
@@ -78,15 +79,16 @@ def tile_hypconvhyperboloid_v_kernel(tc, x, W, b, z, grad_out, out):
         t_cat = small.tile([P, PASSES, PACK], BF16)
         made = []
 
-        def quantise_x(u, j, copy):
-            if (u, j) in made:
-                return
+        def regroup_x(u, j, copy):
             grouped = grouped_bufs[len(made) % GROUPED_BUFS]
             made.append((u, j))
             src, dst = regrouped(x_win[:, u, j : j + PACK, 0:C_IN], grouped[:, 0:C_IN, :])
             copy(out=dst, in_=src)
             if j == T_CAT_TAP[1] and TOP < u < BOTTOM:
                 nc.vector.tensor_copy(out=grouped[:, 0, :], in_=t_cat[:, u - 1, :])
+
+        def quantise_x(u, j):
+            grouped = grouped_bufs[made.index((u, j)) % GROUPED_BUFS]
             nc.vector.quantize_mx(
                 out=x_codes[:, u, j, :].bitcast(E4M3_X4),
                 scales=x_scales[:, u, j, :],
@@ -130,15 +132,31 @@ def tile_hypconvhyperboloid_v_kernel(tc, x, W, b, z, grad_out, out):
             z_sb = dz_in.tile([P, PASSES, PACK, M_ALL], F32)
             g_sb = dz_in.tile([P, PASSES, G_PAD], BF16)
 
-            loaded = []
-            for a in range(PASSES):
-                nc.sync.dma_start(out=z_sb[:, a].rearrange("p t m -> p (t m)"), in_=z_tiles[a])
+            def load_z(a):
+                if a == 0:
+                    for t in range(PACK):
+                        nc.sync.dma_start(out=z_sb[:, a, t, :], in_=z_tiles[a][:, :, t * M_ALL : (t + 1) * M_ALL])
+                else:
+                    nc.sync.dma_start(out=z_sb[:, a].rearrange("p t m -> p (t m)"), in_=z_tiles[a])
+
+            def load_g(a):
                 nc.sync.dma_start(out=g_sb[:, a, 0 : PACK * G_IN], in_=g_tiles[a])
-                for i, j in FIRST_TAPS:
-                    u = a + i
-                    if u < BOTTOM and u not in loaded:
-                        loaded.append(u)
-                        nc.sync.dma_start(out=x_win[:, u, 1 : 1 + PACK, 0:C_IN], in_=x_tiles[u - 1])
+
+            def load_x(u):
+                nc.sync.dma_start(out=x_win[:, u, 1 : 1 + PACK, 0:C_IN], in_=x_tiles[u - 1])
+
+            load_z(0)
+            load_g(0)
+            load_x(1)
+            load_x(2)
+            load_z(1)
+            load_g(1)
+            load_z(2)
+            load_x(3)
+            load_g(2)
+            load_z(3)
+            load_x(4)
+            load_g(3)
             fill_edge_tiles(slice(1, 1 + PACK))
             for pp in range(ROW_PARTS):
                 nc.sync.dma_start(
@@ -162,6 +180,9 @@ def tile_hypconvhyperboloid_v_kernel(tc, x, W, b, z, grad_out, out):
                     )
                 t_out = work.tile([P, PACK], F32)
                 nc.scalar.activation(out=t_out[:], in_=sum_sq[:], func=ACT.Sqrt, bias=1.0)
+                new_tiles = [(a + i, j) for i, j in FIRST_TAPS if (a + i, j) not in made]
+                for u, j in new_tiles:
+                    regroup_x(u, j, nc.scalar.copy)
                 inv_t_out = work.tile([P, PACK], F32)
                 nc.vector.reciprocal(out=inv_t_out[:], in_=t_out[:])
                 slope = work.tile([P, PACK], F32)
@@ -173,15 +194,25 @@ def tile_hypconvhyperboloid_v_kernel(tc, x, W, b, z, grad_out, out):
                         in1=g_tokens[:, t, 1:G_IN], op0=ALU.mult, op1=ALU.add,
                     )
                 dz_grouped = work.tile([P, M_ALL, PACK], BF16, align_bytes=64)
-                src, dst = regrouped(dz_rows[:], dz_grouped[:])
-                nc.vector.tensor_copy(out=dst, in_=src)
+                if a < PASSES - 1:
+                    src, dst = regrouped(dz_rows[:], dz_grouped[:])
+                    nc.vector.tensor_copy(out=dst, in_=src)
+                else:
+                    src, dst = regrouped(dz_rows[:, :, 0:M_HALF], dz_grouped[:, 0:M_HALF, :])
+                    nc.vector.tensor_copy(out=dst, in_=src)
+                    src, dst = regrouped(dz_rows[:, :, M_HALF:M_ALL], dz_grouped[:, M_HALF:M_ALL, :])
+                    nc.scalar.copy(out=dst, in_=src)
+                if a < PASSES - 1:
+                    for u, j in new_tiles:
+                        quantise_x(u, j)
                 nc.vector.quantize_mx(
                     out=dz_codes[:, a, :].bitcast(E5M2_X4),
                     scales=dz_scales[:, a, :],
                     in_=dz_grouped[:].rearrange("p m t -> p (m t)"),
                 )
-                for i, j in FIRST_TAPS:
-                    quantise_x(a + i, j, nc.scalar.copy)
+                if a == PASSES - 1:
+                    for u, j in new_tiles:
+                        quantise_x(u, j)
                 for m in range(M_TILES):
                     for tap in FIRST_TAPS:
                         multiply(first_acc[(tap, m)], tap, m, a, a == 0, a == PASSES - 1)
@@ -198,9 +229,16 @@ def tile_hypconvhyperboloid_v_kernel(tc, x, W, b, z, grad_out, out):
         nc.vector.tensor_tensor(out=sum_taps[:], in0=pair_r[:], in1=sum_q[:, 2 : 2 + PASSES, :], op=ALU.add)
         nc.scalar.activation(out=t_cat[:], in_=sum_taps[:], func=ACT.Sqrt, bias=-8.0)
 
+        later_tiles = []
         for i, j in LATER_TAPS:
             for a in range(PASSES):
-                quantise_x(a + i, j, nc.vector.tensor_copy)
+                if (a + i, j) not in made and (a + i, j) not in later_tiles:
+                    later_tiles.append((a + i, j))
+        for k, tile in enumerate(later_tiles):
+            regroup_x(tile[0], tile[1], nc.vector.tensor_copy)
+            if k > 0:
+                quantise_x(later_tiles[k - 1][0], later_tiles[k - 1][1])
+        quantise_x(later_tiles[-1][0], later_tiles[-1][1])
 
         rows_pool = stack.enter_context(tc.tile_pool(name="rows", bufs=1))
         out_rows = [rows_pool.tile([M_TILE, H_COLS], F32, name="out_rows%d" % m) for m in range(M_TILES)]

@@ -37,7 +37,7 @@ H_COLS = 4096
 STORE_ALIGN = 8
 
 FIRST_TAPS = [(1, 1), (2, 1)]
-LATER_TAPS = [(0, 1), (1, 0), (2, 0), (1, 2), (2, 2), (0, 2), (0, 0)]
+LATER_TAPS = [(0, 1), (1, 0), (2, 0), (0, 0), (1, 2), (2, 2), (0, 2)]
 T_CAT_TAP = (1, 2)
 GROUPED_BUFS = 4
 M_HALF = M_ALL // 2
@@ -205,11 +205,15 @@ def tile_hypconvhyperboloid_v_kernel(tc, x, W, b, z, grad_out, out):
                 if a < PASSES - 1:
                     for u, j in new_tiles:
                         quantise_x(u, j)
-                nc.vector.quantize_mx(
-                    out=dz_codes[:, a, :].bitcast(E5M2_X4),
-                    scales=dz_scales[:, a, :],
-                    in_=dz_grouped[:].rearrange("p m t -> p (m t)"),
-                )
+                    halves = [slice(0, M_ALL)]
+                else:
+                    halves = [slice(0, M_HALF), slice(M_HALF, M_ALL)]
+                for half in halves:
+                    nc.vector.quantize_mx(
+                        out=dz_codes[:, a, half].bitcast(E5M2_X4),
+                        scales=dz_scales[:, a, half],
+                        in_=dz_grouped[:, half, :].rearrange("p m t -> p (m t)"),
+                    )
                 if a == PASSES - 1:
                     for u, j in new_tiles:
                         quantise_x(u, j)
@@ -217,17 +221,18 @@ def tile_hypconvhyperboloid_v_kernel(tc, x, W, b, z, grad_out, out):
                     for tap in FIRST_TAPS:
                         multiply(first_acc[(tap, m)], tap, m, a, a == 0, a == PASSES - 1)
 
-        time_sq = small.tile([P, ROW_TILES, SLOTS], F32)
-        nc.vector.tensor_tensor(out=time_sq[:], in0=x_win[:, :, :, 0], in1=x_win[:, :, :, 0], op=ALU.mult)
-        pair_q = small.tile([P, ROW_TILES, PACK], F32)
-        nc.vector.tensor_tensor(out=pair_q[:], in0=time_sq[:, :, 0:PACK], in1=time_sq[:, :, 1 : 1 + PACK], op=ALU.add)
-        sum_q = small.tile([P, ROW_TILES, PACK], F32)
-        nc.vector.tensor_tensor(out=sum_q[:], in0=pair_q[:], in1=time_sq[:, :, 2 : 2 + PACK], op=ALU.add)
-        pair_r = small.tile([P, PASSES, PACK], F32)
-        nc.vector.tensor_tensor(out=pair_r[:], in0=sum_q[:, 0:PASSES, :], in1=sum_q[:, 1 : 1 + PASSES, :], op=ALU.add)
-        sum_taps = small.tile([P, PASSES, PACK], F32)
-        nc.vector.tensor_tensor(out=sum_taps[:], in0=pair_r[:], in1=sum_q[:, 2 : 2 + PASSES, :], op=ALU.add)
-        nc.scalar.activation(out=t_cat[:], in_=sum_taps[:], func=ACT.Sqrt, bias=-8.0)
+        def make_t_cat():
+            time_sq = small.tile([P, ROW_TILES, SLOTS], F32, name="time_sq")
+            nc.vector.tensor_tensor(out=time_sq[:], in0=x_win[:, :, :, 0], in1=x_win[:, :, :, 0], op=ALU.mult)
+            pair_q = small.tile([P, ROW_TILES, PACK], F32, name="pair_q")
+            nc.vector.tensor_tensor(out=pair_q[:], in0=time_sq[:, :, 0:PACK], in1=time_sq[:, :, 1 : 1 + PACK], op=ALU.add)
+            sum_q = small.tile([P, ROW_TILES, PACK], F32, name="sum_q")
+            nc.vector.tensor_tensor(out=sum_q[:], in0=pair_q[:], in1=time_sq[:, :, 2 : 2 + PACK], op=ALU.add)
+            pair_r = small.tile([P, PASSES, PACK], F32, name="pair_r")
+            nc.vector.tensor_tensor(out=pair_r[:], in0=sum_q[:, 0:PASSES, :], in1=sum_q[:, 1 : 1 + PASSES, :], op=ALU.add)
+            sum_taps = small.tile([P, PASSES, PACK], F32, name="sum_taps")
+            nc.vector.tensor_tensor(out=sum_taps[:], in0=pair_r[:], in1=sum_q[:, 2 : 2 + PASSES, :], op=ALU.add)
+            nc.scalar.activation(out=t_cat[:], in_=sum_taps[:], func=ACT.Sqrt, bias=-8.0)
 
         later_tiles = []
         for i, j in LATER_TAPS:
@@ -235,6 +240,8 @@ def tile_hypconvhyperboloid_v_kernel(tc, x, W, b, z, grad_out, out):
                 if (a + i, j) not in made and (a + i, j) not in later_tiles:
                     later_tiles.append((a + i, j))
         for k, tile in enumerate(later_tiles):
+            if tile == (1, T_CAT_TAP[1]):
+                make_t_cat()
             regroup_x(tile[0], tile[1], nc.vector.tensor_copy)
             if k > 0:
                 quantise_x(later_tiles[k - 1][0], later_tiles[k - 1][1])
@@ -251,21 +258,59 @@ def tile_hypconvhyperboloid_v_kernel(tc, x, W, b, z, grad_out, out):
             nc.scalar.copy(out=out_rows[m][:, first:last], in_=acc[:, 1:C_IN])
             if tap == T_CAT_TAP:
                 nc.scalar.copy(out=out_rows[m][:, 0:1], in_=acc[:, 0:1])
-            left_there = (n - 1 in stored) if n > 0 else (3 * T_CAT_TAP[0] + T_CAT_TAP[1] in stored)
+            t_cat_n = 3 * T_CAT_TAP[0] + T_CAT_TAP[1]
+            left_there = (n - 1 in stored) if n > 0 else (t_cat_n in stored)
             right_there = n + 1 in stored
             lo = first - first % STORE_ALIGN if left_there else first + (-first) % STORE_ALIGN
             hi = last + (-last) % STORE_ALIGN if right_there else last - last % STORE_ALIGN
-            nc.sync.dma_start(out=out[m * M_TILE : (m + 1) * M_TILE, lo:hi], in_=out_rows[m][:, lo:hi])
+            rows = slice(m * M_TILE, (m + 1) * M_TILE)
+            nc.sync.dma_start(out=out[rows, lo:hi], in_=out_rows[m][:, lo:hi])
+            if tap == T_CAT_TAP and 0 in stored:
+                nc.sync.dma_start(out=out[rows, 0:STORE_ALIGN], in_=out_rows[m][:, 0:STORE_ALIGN])
 
-        for tap in FIRST_TAPS:
+        def open_tap():
+            return [psum.tile([M_TILE, N_TILE], F32, name="acc%d" % m, tag="acc") for m in range(M_TILES)]
+
+        def empty_tap(accs, tap):
             for m in range(M_TILES):
-                empty_and_store(first_acc[(tap, m)], tap, m)
-            stored.append(3 * tap[0] + tap[1])
-        for tap in LATER_TAPS:
-            accs = [psum.tile([M_TILE, N_TILE], F32, name="acc%d" % m, tag="acc") for m in range(M_TILES)]
-            passes = sorted(range(PASSES), key=lambda a: made.index((a + tap[0], tap[1])))
-            for m in range(M_TILES):
-                for a in passes:
-                    multiply(accs[m], tap, m, a, a == passes[0], a == passes[-1])
                 empty_and_store(accs[m], tap, m)
             stored.append(3 * tap[0] + tap[1])
+
+        def upper_tap(j, bank_by_bank):
+            tap = (0, j)
+            accs = open_tap()
+            order = [1, 2, 3, 0]
+            if bank_by_bank:
+                for m in range(M_TILES):
+                    for a in order:
+                        multiply(accs[m], tap, m, a, a == order[0], a == order[-1])
+                    empty_and_store(accs[m], tap, m)
+                stored.append(3 * tap[0] + tap[1])
+            else:
+                for a in order:
+                    for m in range(M_TILES):
+                        multiply(accs[m], tap, m, a, a == order[0], a == order[-1])
+                empty_tap(accs, tap)
+
+        def tap_pair(j):
+            middle = open_tap()
+            lower = open_tap()
+            for u in range(1, ROW_TILES):
+                if u - 1 < PASSES:
+                    for m in range(M_TILES):
+                        multiply(middle[m], (1, j), m, u - 1, u - 1 == 0, u - 1 == PASSES - 1)
+                if u - 1 == PASSES - 1:
+                    empty_tap(middle, (1, j))
+                if u - 2 >= 0:
+                    for m in range(M_TILES):
+                        multiply(lower[m], (2, j), m, u - 2, u - 2 == 0, u - 2 == PASSES - 1)
+            empty_tap(lower, (2, j))
+
+        for tap in FIRST_TAPS:
+            empty_tap([first_acc[(tap, m)] for m in range(M_TILES)], tap)
+        with tc.manual_schedule(engines={mybir.EngineType.PE}):
+            upper_tap(1, False)
+            tap_pair(0)
+            upper_tap(0, False)
+            tap_pair(2)
+            upper_tap(2, True)

@@ -148,8 +148,8 @@ def tile_hypconvhyperboloid_v_kernel(tc, x, W, b, z, grad_out, out):
             load_z(0)
             load_g(0)
             load_x(1)
-            load_x(2)
             load_z(1)
+            load_x(2)
             load_g(1)
             load_z(2)
             load_x(3)
@@ -169,57 +169,87 @@ def tile_hypconvhyperboloid_v_kernel(tc, x, W, b, z, grad_out, out):
                 )
             fill_edge_tiles(slice(0, SLOTS, SLOTS - 1))
 
-            for a in range(PASSES):
-                g_tokens = g_sb[:, a, 0 : PACK * G_IN].rearrange("p (t m) -> p t m", t=PACK)
-                squares = work.tile([P, PACK, M_ALL], BF16)
-                sum_sq = work.tile([P, PACK], F32)
+            sum_sq = dz_in.tile([P, PASSES, PACK], F32)
+            t_out = dz_in.tile([P, PASSES, PACK], F32)
+            inv_t_out = dz_in.tile([P, PASSES, PACK], F32)
+            slope = dz_in.tile([P, PASSES, PACK], F32)
+            dz_rows = {}
+            dz_grouped = {}
+
+            def g_tokens(a):
+                return g_sb[:, a, 0 : PACK * G_IN].rearrange("p (t m) -> p t m", t=PACK)
+
+            def norms(a):
+                squares = work.tile([P, PACK, M_ALL], BF16, name="squares")
                 for t in range(PACK):
                     nc.scalar.activation(
                         out=squares[:, t, :], in_=z_sb[:, a, t, :], func=ACT.Square,
-                        accum_out=sum_sq[:, t : t + 1],
+                        accum_out=sum_sq[:, a, t : t + 1],
                     )
-                t_out = work.tile([P, PACK], F32)
-                nc.scalar.activation(out=t_out[:], in_=sum_sq[:], func=ACT.Sqrt, bias=1.0)
-                new_tiles = [(a + i, j) for i, j in FIRST_TAPS if (a + i, j) not in made]
-                for u, j in new_tiles:
-                    regroup_x(u, j, nc.scalar.copy)
-                inv_t_out = work.tile([P, PACK], F32)
-                nc.vector.reciprocal(out=inv_t_out[:], in_=t_out[:])
-                slope = work.tile([P, PACK], F32)
-                nc.vector.tensor_tensor(out=slope[:], in0=g_tokens[:, :, 0], in1=inv_t_out[:], op=ALU.mult)
-                dz_rows = work.tile([P, PACK, M_ALL], BF16)
+                nc.scalar.activation(out=t_out[:, a, :], in_=sum_sq[:, a, :], func=ACT.Sqrt, bias=1.0)
+
+            def slopes(a):
+                nc.vector.reciprocal(out=inv_t_out[:, a, :], in_=t_out[:, a, :])
+                nc.vector.tensor_tensor(out=slope[:, a, :], in0=g_tokens(a)[:, :, 0], in1=inv_t_out[:, a, :], op=ALU.mult)
+
+            def rows(a):
+                dz_rows[a] = work.tile([P, PACK, M_ALL], BF16, name="dz_rows")
                 for t in range(PACK):
                     nc.vector.scalar_tensor_tensor(
-                        out=dz_rows[:, t, :], in0=z_sb[:, a, t, :], scalar=slope[:, t : t + 1],
-                        in1=g_tokens[:, t, 1:G_IN], op0=ALU.mult, op1=ALU.add,
+                        out=dz_rows[a][:, t, :], in0=z_sb[:, a, t, :], scalar=slope[:, a, t : t + 1],
+                        in1=g_tokens(a)[:, t, 1:G_IN], op0=ALU.mult, op1=ALU.add,
                     )
-                dz_grouped = work.tile([P, M_ALL, PACK], BF16, align_bytes=64)
+
+            def regroup_dz(a):
+                dz_grouped[a] = work.tile([P, M_ALL, PACK], BF16, align_bytes=64, name="dz_grouped")
                 if a < PASSES - 1:
-                    src, dst = regrouped(dz_rows[:], dz_grouped[:])
+                    src, dst = regrouped(dz_rows[a][:], dz_grouped[a][:])
                     nc.vector.tensor_copy(out=dst, in_=src)
                 else:
-                    src, dst = regrouped(dz_rows[:, :, 0:M_HALF], dz_grouped[:, 0:M_HALF, :])
+                    src, dst = regrouped(dz_rows[a][:, :, 0:M_HALF], dz_grouped[a][:, 0:M_HALF, :])
                     nc.vector.tensor_copy(out=dst, in_=src)
-                    src, dst = regrouped(dz_rows[:, :, M_HALF:M_ALL], dz_grouped[:, M_HALF:M_ALL, :])
+                    src, dst = regrouped(dz_rows[a][:, :, M_HALF:M_ALL], dz_grouped[a][:, M_HALF:M_ALL, :])
                     nc.scalar.copy(out=dst, in_=src)
-                if a < PASSES - 1:
-                    for u, j in new_tiles:
-                        quantise_x(u, j)
-                    halves = [slice(0, M_ALL)]
-                else:
-                    halves = [slice(0, M_HALF), slice(M_HALF, M_ALL)]
+
+            def quantise_dz(a):
+                halves = [slice(0, M_ALL)] if a < PASSES - 1 else [slice(0, M_HALF), slice(M_HALF, M_ALL)]
                 for half in halves:
                     nc.vector.quantize_mx(
                         out=dz_codes[:, a, half].bitcast(E5M2_X4),
                         scales=dz_scales[:, a, half],
-                        in_=dz_grouped[:, half, :].rearrange("p m t -> p (m t)"),
+                        in_=dz_grouped[a][:, half, :].rearrange("p m t -> p (m t)"),
                     )
-                if a == PASSES - 1:
-                    for u, j in new_tiles:
-                        quantise_x(u, j)
+
+            def first_passes(a):
                 for m in range(M_TILES):
                     for tap in FIRST_TAPS:
                         multiply(first_acc[(tap, m)], tap, m, a, a == 0, a == PASSES - 1)
+
+            with tc.manual_schedule(engines={mybir.EngineType.DVE, mybir.EngineType.Activation}):
+                norms(0)
+                regroup_x(1, 1, nc.scalar.copy)
+                slopes(0)
+                rows(0)
+                regroup_dz(0)
+                norms(1)
+                regroup_x(2, 1, nc.scalar.copy)
+                quantise_x(1, 1)
+                quantise_dz(0)
+                for a in range(1, PASSES):
+                    slopes(a)
+                    if a > 1:
+                        quantise_dz(a - 1)
+                    rows(a)
+                    quantise_x(a + 1, 1)
+                    first_passes(a - 1)
+                    regroup_dz(a)
+                    if a + 1 < PASSES:
+                        norms(a + 1)
+                        regroup_x(a + 2, 1, nc.scalar.copy)
+                quantise_dz(PASSES - 1)
+            regroup_x(BOTTOM, 1, nc.scalar.copy)
+            quantise_x(BOTTOM, 1)
+            first_passes(PASSES - 1)
 
         def make_t_cat():
             time_sq = small.tile([P, ROW_TILES, SLOTS], F32, name="time_sq")

@@ -17,6 +17,7 @@ ALU = mybir.AluOpType
 P = 128
 PACK = 4
 ROW_PARTS = 8
+SPREAD = 4
 IMAGES = 4
 IMAGE_PARTS = 32
 PASSES = 4
@@ -137,10 +138,16 @@ def tile_hypconvhyperboloid_v_kernel(tc, x, W, b, z, grad_out, out):
                     for t in range(PACK):
                         nc.sync.dma_start(out=z_sb[:, a, t, :], in_=z_tiles[a][:, :, t * M_ALL : (t + 1) * M_ALL])
                 else:
-                    nc.sync.dma_start(out=z_sb[:, a].rearrange("p t m -> p (t m)"), in_=z_tiles[a])
+                    for c in range(SPREAD):
+                        nc.sync.dma_start(
+                            out=z_sb[c:P:SPREAD, a].rearrange("p t m -> p (t m)"), in_=z_tiles[a][:, c:ROW_PARTS:SPREAD, :]
+                        )
 
             def load_g(a):
-                nc.sync.dma_start(out=g_sb[:, a, 0 : PACK * G_IN], in_=g_tiles[a])
+                for c in range(SPREAD):
+                    nc.sync.dma_start(
+                        out=g_sb[c:P:SPREAD, a, 0 : PACK * G_IN], in_=g_tiles[a][:, c:ROW_PARTS:SPREAD, :]
+                    )
 
             def load_x(u):
                 nc.sync.dma_start(out=x_win[:, u, 1 : 1 + PACK, 0:C_IN], in_=x_tiles[u - 1])

@@ -152,18 +152,19 @@ def tile_hypconvhyperboloid_v_kernel(tc, x, W, b, z, grad_out, out):
             def load_x(u):
                 nc.sync.dma_start(out=x_win[:, u, 1 : 1 + PACK, 0:C_IN], in_=x_tiles[u - 1])
 
-            load_z(0)
-            load_g(0)
-            load_x(1)
-            load_z(1)
-            load_x(2)
-            load_g(1)
-            load_z(2)
-            load_x(3)
-            load_g(2)
-            load_z(3)
-            load_x(4)
-            load_g(3)
+            with tc.manual_schedule(engines={mybir.EngineType.SP}):
+                load_z(0)
+                load_g(0)
+                load_x(1)
+                load_z(1)
+                load_x(2)
+                load_g(1)
+                load_z(2)
+                load_x(3)
+                load_g(2)
+                load_z(3)
+                load_x(4)
+                load_g(3)
             fill_edge_tiles(slice(1, 1 + PACK))
             for pp in range(ROW_PARTS):
                 nc.sync.dma_start(

@@ -130,23 +130,23 @@ def tile_hypconvhyperboloid_v_kernel(tc, x, W, b, z, grad_out, out):
                 )
 
         with tc.tile_pool(name="dz_work", bufs=2) as work, tc.tile_pool(name="dz_in", bufs=1) as dz_in:
-            z_sb = dz_in.tile([P, PASSES, PACK, M_ALL], F32)
-            g_sb = dz_in.tile([P, PASSES, G_PAD], BF16)
+            z_sb = [dz_in.tile([P, PACK, M_ALL], F32, name="z_sb%d" % a) for a in range(PASSES)]
+            g_sb = [dz_in.tile([P, G_PAD], BF16, name="g_sb%d" % a) for a in range(PASSES)]
 
             def load_z(a):
                 if a == 0:
                     for t in range(PACK):
-                        nc.sync.dma_start(out=z_sb[:, a, t, :], in_=z_tiles[a][:, :, t * M_ALL : (t + 1) * M_ALL])
+                        nc.sync.dma_start(out=z_sb[a][:, t, :], in_=z_tiles[a][:, :, t * M_ALL : (t + 1) * M_ALL])
                 else:
                     for c in range(SPREAD):
                         nc.sync.dma_start(
-                            out=z_sb[c:P:SPREAD, a].rearrange("p t m -> p (t m)"), in_=z_tiles[a][:, c:ROW_PARTS:SPREAD, :]
+                            out=z_sb[a][c:P:SPREAD].rearrange("p t m -> p (t m)"), in_=z_tiles[a][:, c:ROW_PARTS:SPREAD, :]
                         )
 
             def load_g(a):
                 for c in range(SPREAD):
                     nc.sync.dma_start(
-                        out=g_sb[c:P:SPREAD, a, 0 : PACK * G_IN], in_=g_tiles[a][:, c:ROW_PARTS:SPREAD, :]
+                        out=g_sb[a][c:P:SPREAD, 0 : PACK * G_IN], in_=g_tiles[a][:, c:ROW_PARTS:SPREAD, :]
                     )
 
             def load_x(u):
@@ -165,17 +165,17 @@ def tile_hypconvhyperboloid_v_kernel(tc, x, W, b, z, grad_out, out):
                 load_z(3)
                 load_x(4)
                 load_g(3)
-            fill_edge_tiles(slice(1, 1 + PACK))
-            for pp in range(ROW_PARTS):
-                nc.sync.dma_start(
-                    out=x_win[pp:P:ROW_PARTS, 1 : 1 + PASSES, 0, 0:C_IN],
-                    in_=x_pixels[max(PACK * pp - 1, 0)],
-                )
-                nc.sync.dma_start(
-                    out=x_win[pp:P:ROW_PARTS, 1 : 1 + PASSES, SLOTS - 1, 0:C_IN],
-                    in_=x_pixels[min(PACK * pp + PACK, 31)],
-                )
-            fill_edge_tiles(slice(0, SLOTS, SLOTS - 1))
+                fill_edge_tiles(slice(1, 1 + PACK))
+                for pp in range(ROW_PARTS):
+                    nc.sync.dma_start(
+                        out=x_win[pp:P:ROW_PARTS, 1 : 1 + PASSES, 0, 0:C_IN],
+                        in_=x_pixels[max(PACK * pp - 1, 0)],
+                    )
+                    nc.sync.dma_start(
+                        out=x_win[pp:P:ROW_PARTS, 1 : 1 + PASSES, SLOTS - 1, 0:C_IN],
+                        in_=x_pixels[min(PACK * pp + PACK, 31)],
+                    )
+                fill_edge_tiles(slice(0, SLOTS, SLOTS - 1))
 
             sum_sq = dz_in.tile([P, PASSES, PACK], F32)
             t_out = dz_in.tile([P, PASSES, PACK], F32)
@@ -185,13 +185,13 @@ def tile_hypconvhyperboloid_v_kernel(tc, x, W, b, z, grad_out, out):
             dz_grouped = {}
 
             def g_tokens(a):
-                return g_sb[:, a, 0 : PACK * G_IN].rearrange("p (t m) -> p t m", t=PACK)
+                return g_sb[a][:, 0 : PACK * G_IN].rearrange("p (t m) -> p t m", t=PACK)
 
             def norms(a):
                 squares = work.tile([P, PACK, M_ALL], BF16, name="squares")
                 for t in range(PACK):
                     nc.scalar.activation(
-                        out=squares[:, t, :], in_=z_sb[:, a, t, :], func=ACT.Square,
+                        out=squares[:, t, :], in_=z_sb[a][:, t, :], func=ACT.Square,
                         accum_out=sum_sq[:, a, t : t + 1],
                     )
                 nc.scalar.activation(out=t_out[:, a, :], in_=sum_sq[:, a, :], func=ACT.Sqrt, bias=1.0)
@@ -204,7 +204,7 @@ def tile_hypconvhyperboloid_v_kernel(tc, x, W, b, z, grad_out, out):
                 dz_rows[a] = work.tile([P, PACK, M_ALL], BF16, name="dz_rows")
                 for t in range(PACK):
                     nc.vector.scalar_tensor_tensor(
-                        out=dz_rows[a][:, t, :], in0=z_sb[:, a, t, :], scalar=slope[:, a, t : t + 1],
+                        out=dz_rows[a][:, t, :], in0=z_sb[a][:, t, :], scalar=slope[:, a, t : t + 1],
                         in1=g_tokens(a)[:, t, 1:G_IN], op0=ALU.mult, op1=ALU.add,
                     )
 

@@ -134,13 +134,11 @@ def tile_hypconvhyperboloid_v_kernel(tc, x, W, b, z, grad_out, out):
             g_sb = [dz_in.tile([P, G_PAD], BF16, name="g_sb%d" % a) for a in range(PASSES)]
 
             def load_z(a):
-                if a == 0:
-                    for t in range(PACK):
-                        nc.sync.dma_start(out=z_sb[a][:, t, :], in_=z_tiles[a][:, :, t * M_ALL : (t + 1) * M_ALL])
-                else:
+                for t in range(0, PACK, 2):
                     for c in range(SPREAD):
                         nc.sync.dma_start(
-                            out=z_sb[a][c:P:SPREAD].rearrange("p t m -> p (t m)"), in_=z_tiles[a][:, c:ROW_PARTS:SPREAD, :]
+                            out=z_sb[a][c:P:SPREAD, t : t + 2].rearrange("p t m -> p (t m)"),
+                            in_=z_tiles[a][:, c:ROW_PARTS:SPREAD, t * M_ALL : (t + 2) * M_ALL],
                         )
 
             def load_g(a):
@@ -150,7 +148,10 @@ def tile_hypconvhyperboloid_v_kernel(tc, x, W, b, z, grad_out, out):
                     )
 
             def load_x(u):
-                nc.sync.dma_start(out=x_win[:, u, 1 : 1 + PACK, 0:C_IN], in_=x_tiles[u - 1])
+                for t in range(PACK):
+                    nc.sync.dma_start(
+                        out=x_win[:, u, 1 + t, 0:C_IN], in_=x_tiles[u - 1][:, :, t * C_IN : (t + 1) * C_IN]
+                    )
 
             with tc.manual_schedule(engines={mybir.EngineType.SP}):
                 load_z(0)

@@ -172,6 +172,7 @@ def tile_hypconvhyperboloid_v_kernel(tc, x, W, b, z, grad_out, out):
                         out=x_win[pp:P:ROW_PARTS, 1 : 1 + PASSES, 0, 0:C_IN],
                         in_=x_pixels[max(PACK * pp - 1, 0)],
                     )
+                for pp in range(ROW_PARTS):
                     nc.sync.dma_start(
                         out=x_win[pp:P:ROW_PARTS, 1 : 1 + PASSES, SLOTS - 1, 0:C_IN],
                         in_=x_pixels[min(PACK * pp + PACK, 31)],
@@ -197,8 +198,10 @@ def tile_hypconvhyperboloid_v_kernel(tc, x, W, b, z, grad_out, out):
                     )
                 nc.scalar.activation(out=t_out[:, a, :], in_=sum_sq[:, a, :], func=ACT.Sqrt, bias=1.0)
 
-            def slopes(a):
+            def inverses(a):
                 nc.vector.reciprocal(out=inv_t_out[:, a, :], in_=t_out[:, a, :])
+
+            def slopes(a):
                 nc.vector.tensor_tensor(out=slope[:, a, :], in0=g_tokens(a)[:, :, 0], in1=inv_t_out[:, a, :], op=ALU.mult)
 
             def rows(a):
@@ -220,34 +223,39 @@ def tile_hypconvhyperboloid_v_kernel(tc, x, W, b, z, grad_out, out):
                     src, dst = regrouped(dz_rows[a][:, :, M_HALF:M_ALL], dz_grouped[a][:, M_HALF:M_ALL, :])
                     nc.scalar.copy(out=dst, in_=src)
 
-            def quantise_dz(a):
-                halves = [slice(0, M_ALL)] if a < PASSES - 1 else [slice(0, M_HALF), slice(M_HALF, M_ALL)]
-                for half in halves:
-                    nc.vector.quantize_mx(
-                        out=dz_codes[:, a, half].bitcast(E5M2_X4),
-                        scales=dz_scales[:, a, half],
-                        in_=dz_grouped[a][:, half, :].rearrange("p m t -> p (m t)"),
-                    )
+            def quantise_dz(a, half):
+                cols = slice(half * M_HALF, (half + 1) * M_HALF)
+                nc.vector.quantize_mx(
+                    out=dz_codes[:, a, cols].bitcast(E5M2_X4),
+                    scales=dz_scales[:, a, cols],
+                    in_=dz_grouped[a][:, cols, :].rearrange("p m t -> p (m t)"),
+                )
 
             def first_passes(a):
                 for m in range(M_TILES):
                     for tap in FIRST_TAPS:
-                        multiply(first_acc[(tap, m)], tap, m, a, a == 0, a == PASSES - 1)
+                        multiply(first_acc[(tap, m)], tap, m, a, a == 0, False)
 
             with tc.manual_schedule(engines={mybir.EngineType.DVE, mybir.EngineType.Activation}):
                 norms(0)
                 regroup_x(1, 1, nc.scalar.copy)
+                inverses(0)
                 slopes(0)
                 rows(0)
                 regroup_dz(0)
                 norms(1)
                 regroup_x(2, 1, nc.scalar.copy)
                 quantise_x(1, 1)
-                quantise_dz(0)
+                quantise_dz(0, 0)
                 for a in range(1, PASSES):
+                    inverses(a)
+                    if a > 1:
+                        quantise_dz(a - 1, 0)
+                    else:
+                        quantise_dz(0, 1)
                     slopes(a)
                     if a > 1:
-                        quantise_dz(a - 1)
+                        quantise_dz(a - 1, 1)
                     rows(a)
                     quantise_x(a + 1, 1)
                     first_passes(a - 1)
@@ -255,10 +263,10 @@ def tile_hypconvhyperboloid_v_kernel(tc, x, W, b, z, grad_out, out):
                     if a + 1 < PASSES:
                         norms(a + 1)
                         regroup_x(a + 2, 1, nc.scalar.copy)
-                quantise_dz(PASSES - 1)
+                quantise_dz(PASSES - 1, 0)
+                quantise_dz(PASSES - 1, 1)
             regroup_x(BOTTOM, 1, nc.scalar.copy)
             quantise_x(BOTTOM, 1)
-            first_passes(PASSES - 1)
 
         def make_t_cat():
             time_sq = small.tile([P, ROW_TILES, SLOTS], F32, name="time_sq")
@@ -345,10 +353,22 @@ def tile_hypconvhyperboloid_v_kernel(tc, x, W, b, z, grad_out, out):
                         multiply(lower[m], (2, j), m, u - 2, u - 2 == 0, u - 2 == PASSES - 1)
             empty_tap(lower, (2, j))
 
-        for tap in FIRST_TAPS:
-            empty_tap([first_acc[(tap, m)] for m in range(M_TILES)], tap)
+        def close_first_tap(tap):
+            accs = [first_acc[(tap, m)] for m in range(M_TILES)]
+            for m in range(M_TILES):
+                multiply(accs[m], tap, m, PASSES - 1, False, True)
+            empty_tap(accs, tap)
+
         with tc.manual_schedule(engines={mybir.EngineType.PE}):
-            upper_tap(1, False)
+            close_first_tap((1, 1))
+            upper = open_tap()
+            for a in range(1, PASSES):
+                for m in range(M_TILES):
+                    multiply(upper[m], (0, 1), m, a, a == 1, False)
+            close_first_tap((2, 1))
+            for m in range(M_TILES):
+                multiply(upper[m], (0, 1), m, 0, False, True)
+            empty_tap(upper, (0, 1))
             tap_pair(0)
             upper_tap(0, False)
             tap_pair(2)

@@ -246,16 +246,11 @@ def tile_hypconvhyperboloid_v_kernel(tc, x, W, b, z, grad_out, out):
                 norms(1)
                 regroup_x(2, 1, nc.scalar.copy)
                 quantise_x(1, 1)
-                quantise_dz(0, 0)
                 for a in range(1, PASSES):
                     inverses(a)
-                    if a > 1:
-                        quantise_dz(a - 1, 0)
-                    else:
-                        quantise_dz(0, 1)
+                    quantise_dz(a - 1, 0)
                     slopes(a)
-                    if a > 1:
-                        quantise_dz(a - 1, 1)
+                    quantise_dz(a - 1, 1)
                     rows(a)
                     quantise_x(a + 1, 1)
                     first_passes(a - 1)
@@ -265,8 +260,6 @@ def tile_hypconvhyperboloid_v_kernel(tc, x, W, b, z, grad_out, out):
                         regroup_x(a + 2, 1, nc.scalar.copy)
                 quantise_dz(PASSES - 1, 0)
                 quantise_dz(PASSES - 1, 1)
-            regroup_x(BOTTOM, 1, nc.scalar.copy)
-            quantise_x(BOTTOM, 1)
 
         def make_t_cat():
             time_sq = small.tile([P, ROW_TILES, SLOTS], F32, name="time_sq")
@@ -281,7 +274,7 @@ def tile_hypconvhyperboloid_v_kernel(tc, x, W, b, z, grad_out, out):
             nc.vector.tensor_tensor(out=sum_taps[:], in0=pair_r[:], in1=sum_q[:, 2 : 2 + PASSES, :], op=ALU.add)
             nc.scalar.activation(out=t_cat[:], in_=sum_taps[:], func=ACT.Sqrt, bias=-8.0)
 
-        later_tiles = []
+        later_tiles = [(BOTTOM, 1)]
         for i, j in LATER_TAPS:
             for a in range(PASSES):
                 if (a + i, j) not in made and (a + i, j) not in later_tiles:
@@ -298,21 +291,22 @@ def tile_hypconvhyperboloid_v_kernel(tc, x, W, b, z, grad_out, out):
         out_rows = [rows_pool.tile([M_TILE, H_COLS], F32, name="out_rows%d" % m) for m in range(M_TILES)]
         stored = []
 
-        def empty_and_store(acc, tap, m):
+        def empty_and_store(acc, tap, m, cuts=()):
             n = 3 * tap[0] + tap[1]
             first = 1 + SPACE * n
             last = first + SPACE
-            nc.scalar.copy(out=out_rows[m][:, first:last], in_=acc[:, 1:C_IN])
-            if tap == T_CAT_TAP:
-                nc.scalar.copy(out=out_rows[m][:, 0:1], in_=acc[:, 0:1])
             t_cat_n = 3 * T_CAT_TAP[0] + T_CAT_TAP[1]
             left_there = (n - 1 in stored) if n > 0 else (t_cat_n in stored)
             right_there = n + 1 in stored
             lo = first - first % STORE_ALIGN if left_there else first + (-first) % STORE_ALIGN
             hi = last + (-last) % STORE_ALIGN if right_there else last - last % STORE_ALIGN
             rows = slice(m * M_TILE, (m + 1) * M_TILE)
-            nc.sync.dma_start(out=out[rows, lo:hi], in_=out_rows[m][:, lo:hi])
-            if tap == T_CAT_TAP and 0 in stored:
+            for a, b in zip([first, *cuts], [*cuts, last]):
+                nc.scalar.copy(out=out_rows[m][:, a:b], in_=acc[:, 1 + a - first : 1 + b - first])
+                store = slice(lo if a == first else a, hi if b == last else b)
+                nc.sync.dma_start(out=out[rows, store], in_=out_rows[m][:, store])
+            if tap == T_CAT_TAP:
+                nc.scalar.copy(out=out_rows[m][:, 0:1], in_=acc[:, 0:1])
                 nc.sync.dma_start(out=out[rows, 0:STORE_ALIGN], in_=out_rows[m][:, 0:STORE_ALIGN])
 
         def open_tap():
@@ -331,7 +325,9 @@ def tile_hypconvhyperboloid_v_kernel(tc, x, W, b, z, grad_out, out):
                 for m in range(M_TILES):
                     for a in order:
                         multiply(accs[m], tap, m, a, a == order[0], a == order[-1])
-                    empty_and_store(accs[m], tap, m)
+                    middle = 1 + SPACE * (3 * tap[0] + tap[1]) + SPACE // 2
+                    cuts = [middle - middle % STORE_ALIGN] if m == M_TILES - 1 else []
+                    empty_and_store(accs[m], tap, m, cuts)
                 stored.append(3 * tap[0] + tap[1])
             else:
                 for a in order:
@@ -362,8 +358,8 @@ def tile_hypconvhyperboloid_v_kernel(tc, x, W, b, z, grad_out, out):
         with tc.manual_schedule(engines={mybir.EngineType.PE}):
             close_first_tap((1, 1))
             upper = open_tap()
-            for a in range(1, PASSES):
-                for m in range(M_TILES):
+            for m in range(M_TILES):
+                for a in range(1, PASSES):
                     multiply(upper[m], (0, 1), m, a, a == 1, False)
             close_first_tap((2, 1))
             for m in range(M_TILES):

@@ -28,6 +28,7 @@ SLOTS = PACK + 2
 C_IN = 456
 C_PAD = 464
 SPACE = C_IN - 1
+OWN = slice(1, 1 + PACK)
 G_IN = 513
 G_PAD = 2064
 M_ALL = 512
@@ -54,7 +55,6 @@ def tile_hypconvhyperboloid_v_kernel(tc, x, W, b, z, grad_out, out):
     z_tiles = z.rearrange("b (rh a) (pp t) m -> a (b rh) pp (t m)", a=PASSES, t=PACK)
     g_tiles = grad_out.rearrange("b (rh a) (pp t) m -> a (b rh) pp (t m)", a=PASSES, t=PACK)
     x_tiles = x.rearrange("b (rh a) (pp t) c -> a (b rh) pp (t c)", a=PASSES, t=PACK)
-    x_pixels = x.rearrange("b (rh a) q c -> q (b rh) a c", a=PASSES)
 
     with ExitStack() as stack:
         keep = stack.enter_context(tc.tile_pool(name="keep", bufs=1))
@@ -109,18 +109,38 @@ def tile_hypconvhyperboloid_v_kernel(tc, x, W, b, z, grad_out, out):
                 stop=stop,
             )
 
-        def fill_edge_tiles(slots):
+        def shift_pixels(slot, tiles):
+            source, step = (PACK, -1) if slot == 0 else (1, 1)
+            for first, last in [(0, P - ROW_PARTS), (P - ROW_PARTS, P - 1)]:
+                lower, upper = slice(first, last), slice(first + 1, last + 1)
+                to, take = (upper, lower) if step < 0 else (lower, upper)
+                nc.sync.dma_start(out=x_win[to, tiles, slot, 0:C_IN], in_=x_win[take, tiles, source, 0:C_IN])
+
+        def mend_pixels(slot, tiles):
+            end, own = (0, 1) if slot == 0 else (ROW_PARTS - 1, PACK)
             nc.sync.dma_start(
-                out=x_win[ROW_PARTS:P, TOP, slots, 0:C_IN], in_=x_win[0 : P - ROW_PARTS, PASSES, slots, 0:C_IN]
+                out=x_win[end:P:ROW_PARTS, tiles, slot, 0:C_IN], in_=x_win[end:P:ROW_PARTS, tiles, own, 0:C_IN]
             )
+
+        def shift_top():
             nc.sync.dma_start(
-                out=x_win[0 : P - ROW_PARTS, BOTTOM, slots, 0:C_IN], in_=x_win[ROW_PARTS:P, 1, slots, 0:C_IN]
+                out=x_win[ROW_PARTS:P, TOP, OWN, 0:C_IN], in_=x_win[0 : P - ROW_PARTS, PASSES, OWN, 0:C_IN]
             )
+
+        def shift_bottom():
+            nc.sync.dma_start(
+                out=x_win[0 : P - ROW_PARTS, BOTTOM, OWN, 0:C_IN], in_=x_win[ROW_PARTS:P, 1, OWN, 0:C_IN]
+            )
+
+        def mend_top():
             for image in range(IMAGES):
                 first = slice(image * IMAGE_PARTS, image * IMAGE_PARTS + ROW_PARTS)
+                nc.sync.dma_start(out=x_win[first, TOP, OWN, 0:C_IN], in_=x_win[first, 1, OWN, 0:C_IN])
+
+        def mend_bottom():
+            for image in range(IMAGES):
                 last = slice((image + 1) * IMAGE_PARTS - ROW_PARTS, (image + 1) * IMAGE_PARTS)
-                nc.sync.dma_start(out=x_win[first, TOP, slots, 0:C_IN], in_=x_win[first, 1, slots, 0:C_IN])
-                nc.sync.dma_start(out=x_win[last, BOTTOM, slots, 0:C_IN], in_=x_win[last, PASSES, slots, 0:C_IN])
+                nc.sync.dma_start(out=x_win[last, BOTTOM, OWN, 0:C_IN], in_=x_win[last, PASSES, OWN, 0:C_IN])
 
         first_acc = {}
         for tap in FIRST_TAPS:
@@ -165,19 +185,20 @@ def tile_hypconvhyperboloid_v_kernel(tc, x, W, b, z, grad_out, out):
                 load_g(2)
                 load_z(3)
                 load_x(4)
+                shift_bottom()
                 load_g(3)
-                fill_edge_tiles(slice(1, 1 + PACK))
-                for pp in range(ROW_PARTS):
-                    nc.sync.dma_start(
-                        out=x_win[pp:P:ROW_PARTS, 1 : 1 + PASSES, 0, 0:C_IN],
-                        in_=x_pixels[max(PACK * pp - 1, 0)],
-                    )
-                for pp in range(ROW_PARTS):
-                    nc.sync.dma_start(
-                        out=x_win[pp:P:ROW_PARTS, 1 : 1 + PASSES, SLOTS - 1, 0:C_IN],
-                        in_=x_pixels[min(PACK * pp + PACK, 31)],
-                    )
-                fill_edge_tiles(slice(0, SLOTS, SLOTS - 1))
+                inner_tiles, edge_tiles = slice(1, 1 + PASSES), slice(TOP, ROW_TILES, BOTTOM)
+                shift_top()
+                mend_bottom()
+                shift_pixels(0, inner_tiles)
+                mend_top()
+                mend_pixels(0, inner_tiles)
+                shift_pixels(SLOTS - 1, inner_tiles)
+                mend_pixels(SLOTS - 1, inner_tiles)
+                shift_pixels(0, edge_tiles)
+                shift_pixels(SLOTS - 1, edge_tiles)
+                mend_pixels(0, edge_tiles)
+                mend_pixels(SLOTS - 1, edge_tiles)
 
             sum_sq = dz_in.tile([P, PASSES, PACK], F32)
             t_out = dz_in.tile([P, PASSES, PACK], F32)

from contextlib import ExitStack

import concourse.mybir as mybir

FLOPS = 2 * 2048 * 512 * 4096
BYTES = 2 * 2048 * 456 + 4 * 2048 * 512 + 2 * 2048 * 513 + 4 * 512 * 4096

F32 = mybir.dt.float32
BF16 = mybir.dt.bfloat16
U32 = mybir.dt.uint32
U8 = mybir.dt.uint8
E4M3_X4 = mybir.dt.float8_e4m3fn_x4
E5M2_X4 = mybir.dt.float8_e5m2_x4
ACT = mybir.ActivationFunctionType
ALU = mybir.AluOpType

P = 128
PACK = 4
ROW_PARTS = 8
SPREAD = 4
IMAGES = 4
IMAGE_PARTS = 32
PASSES = 4
TOP = 0
BOTTOM = PASSES + 1
ROW_TILES = PASSES + 2
SLOTS = PACK + 2
C_IN = 456
C_PAD = 464
SPACE = C_IN - 1
OWN = slice(1, 1 + PACK)
G_IN = 513
G_PAD = 2064
M_ALL = 512
M_TILE = 128
M_TILES = M_ALL // M_TILE
N_TILE = 512
H_COLS = 4096
STORE_ALIGN = 8

FIRST_TAPS = [(1, 1), (2, 1)]
LATER_TAPS = [(0, 1), (1, 0), (2, 0), (0, 0), (1, 2), (2, 2), (0, 2)]
T_CAT_TAP = (1, 2)
GROUPED_BUFS = 4
M_HALF = M_ALL // 2


def regrouped(rows, grouped):
    return rows.rearrange("p t c -> p c t"), grouped


def tile_hypconvhyperboloid_v_kernel(tc, x, W, b, z, grad_out, out):
    nc = tc.nc

    z_tiles = z.rearrange("b (rh a) (pp t) m -> a (b rh) pp (t m)", a=PASSES, t=PACK)
    g_tiles = grad_out.rearrange("b (rh a) (pp t) m -> a (b rh) pp (t m)", a=PASSES, t=PACK)
    x_tiles = x.rearrange("b (rh a) (pp t) c -> a (b rh) pp (t c)", a=PASSES, t=PACK)

    with ExitStack() as stack:
        keep = stack.enter_context(tc.tile_pool(name="keep", bufs=1))
        small = stack.enter_context(tc.tile_pool(name="small", bufs=1))
        psum = stack.enter_context(tc.psum_pool(name="psum", bufs=8))

        x_win = keep.tile([P, ROW_TILES, SLOTS, C_PAD], BF16)
        x_codes = keep.tile([P, ROW_TILES, 3, N_TILE], U32, align_bytes=64)
        x_scales = keep.tile([P, ROW_TILES, 3, N_TILE], U8, align_bytes=64)
        dz_codes = keep.tile([P, PASSES, M_ALL], U32, align_bytes=64)
        dz_scales = keep.tile([P, PASSES, M_ALL], U8, align_bytes=64)
        grouped_bufs = [
            keep.tile([P, N_TILE, PACK], BF16, align_bytes=64, name="grouped%d" % k)
            for k in range(GROUPED_BUFS)
        ]
        for grouped in grouped_bufs:
            nc.vector.memset(grouped[:, C_IN:N_TILE, :], 0.0)

        one = small.tile([P, 1], F32)
        nc.vector.memset(one[:], 1.0)
        nc.scalar.activation(out=one[:], in_=one[:], func=ACT.Sqrt)

        t_cat = small.tile([P, PASSES, PACK], BF16)
        made = []

        def regroup_x(u, j, copy):
            grouped = grouped_bufs[len(made) % GROUPED_BUFS]
            made.append((u, j))
            src, dst = regrouped(x_win[:, u, j : j + PACK, 0:C_IN], grouped[:, 0:C_IN, :])
            copy(out=dst, in_=src)
            if j == T_CAT_TAP[1] and TOP < u < BOTTOM:
                nc.vector.tensor_copy(out=grouped[:, 0, :], in_=t_cat[:, u - 1, :])

        def quantise_x(u, j):
            grouped = grouped_bufs[made.index((u, j)) % GROUPED_BUFS]
            nc.vector.quantize_mx(
                out=x_codes[:, u, j, :].bitcast(E4M3_X4),
                scales=x_scales[:, u, j, :],
                in_=grouped[:].rearrange("p c t -> p (c t)"),
            )

        def multiply(acc, tap, m, a, start, stop):
            i, j = tap
            m_cols = slice(m * M_TILE, (m + 1) * M_TILE)
            nc.tensor.matmul_mx(
                out=acc[:],
                lhsT=dz_codes[:, a, m_cols].bitcast(E5M2_X4),
                lhsT_scale=dz_scales[:, a, m_cols],
                rhs=x_codes[:, a + i, j, :].bitcast(E4M3_X4),
                rhs_scale=x_scales[:, a + i, j, :],
                start=start,
                stop=stop,
            )

        def shift_pixels(slot, tiles):
            source, step = (PACK, -1) if slot == 0 else (1, 1)
            for first, last in [(0, P - ROW_PARTS), (P - ROW_PARTS, P - 1)]:
                lower, upper = slice(first, last), slice(first + 1, last + 1)
                to, take = (upper, lower) if step < 0 else (lower, upper)
                nc.sync.dma_start(out=x_win[to, tiles, slot, 0:C_IN], in_=x_win[take, tiles, source, 0:C_IN])

        def mend_pixels(slot, tiles):
            end, own = (0, 1) if slot == 0 else (ROW_PARTS - 1, PACK)
            nc.sync.dma_start(
                out=x_win[end:P:ROW_PARTS, tiles, slot, 0:C_IN], in_=x_win[end:P:ROW_PARTS, tiles, own, 0:C_IN]
            )

        def shift_top():
            nc.sync.dma_start(
                out=x_win[ROW_PARTS:P, TOP, OWN, 0:C_IN], in_=x_win[0 : P - ROW_PARTS, PASSES, OWN, 0:C_IN]
            )

        def shift_bottom():
            nc.sync.dma_start(
                out=x_win[0 : P - ROW_PARTS, BOTTOM, OWN, 0:C_IN], in_=x_win[ROW_PARTS:P, 1, OWN, 0:C_IN]
            )

        def mend_top():
            for image in range(IMAGES):
                first = slice(image * IMAGE_PARTS, image * IMAGE_PARTS + ROW_PARTS)
                nc.sync.dma_start(out=x_win[first, TOP, OWN, 0:C_IN], in_=x_win[first, 1, OWN, 0:C_IN])

        def mend_bottom():
            for image in range(IMAGES):
                last = slice((image + 1) * IMAGE_PARTS - ROW_PARTS, (image + 1) * IMAGE_PARTS)
                nc.sync.dma_start(out=x_win[last, BOTTOM, OWN, 0:C_IN], in_=x_win[last, PASSES, OWN, 0:C_IN])

        first_acc = {}
        for tap in FIRST_TAPS:
            for m in range(M_TILES):
                first_acc[(tap, m)] = psum.tile(
                    [M_TILE, N_TILE], F32, name="acc_first_%d_%d" % (tap[0], m), tag="acc"
                )

        with tc.tile_pool(name="dz_work", bufs=2) as work, tc.tile_pool(name="dz_in", bufs=1) as dz_in:
            z_sb = [dz_in.tile([P, PACK, M_ALL], F32, name="z_sb%d" % a) for a in range(PASSES)]
            g_sb = [dz_in.tile([P, G_PAD], BF16, name="g_sb%d" % a) for a in range(PASSES)]

            def load_z(a):
                for t in range(0, PACK, 2):
                    for c in range(SPREAD):
                        nc.sync.dma_start(
                            out=z_sb[a][c:P:SPREAD, t : t + 2].rearrange("p t m -> p (t m)"),
                            in_=z_tiles[a][:, c:ROW_PARTS:SPREAD, t * M_ALL : (t + 2) * M_ALL],
                        )

            def load_g(a):
                for c in range(SPREAD):
                    nc.sync.dma_start(
                        out=g_sb[a][c:P:SPREAD, 0 : PACK * G_IN], in_=g_tiles[a][:, c:ROW_PARTS:SPREAD, :]
                    )

            def load_x(u):
                for t in range(PACK):
                    nc.sync.dma_start(
                        out=x_win[:, u, 1 + t, 0:C_IN], in_=x_tiles[u - 1][:, :, t * C_IN : (t + 1) * C_IN]
                    )

            with tc.manual_schedule(engines={mybir.EngineType.SP}):
                load_z(0)
                load_g(0)
                load_x(1)
                load_z(1)
                load_x(2)
                load_g(1)
                load_z(2)
                load_x(3)
                load_g(2)
                load_z(3)
                load_x(4)
                shift_bottom()
                load_g(3)
                inner_tiles, edge_tiles = slice(1, 1 + PASSES), slice(TOP, ROW_TILES, BOTTOM)
                shift_top()
                mend_bottom()
                shift_pixels(0, inner_tiles)
                mend_top()
                mend_pixels(0, inner_tiles)
                shift_pixels(SLOTS - 1, inner_tiles)
                mend_pixels(SLOTS - 1, inner_tiles)
                shift_pixels(0, edge_tiles)
                shift_pixels(SLOTS - 1, edge_tiles)
                mend_pixels(0, edge_tiles)
                mend_pixels(SLOTS - 1, edge_tiles)

            sum_sq = dz_in.tile([P, PASSES, PACK], F32)
            t_out = dz_in.tile([P, PASSES, PACK], F32)
            inv_t_out = dz_in.tile([P, PASSES, PACK], F32)
            slope = dz_in.tile([P, PASSES, PACK], F32)
            dz_rows = {}
            dz_grouped = {}

            def g_tokens(a):
                return g_sb[a][:, 0 : PACK * G_IN].rearrange("p (t m) -> p t m", t=PACK)

            def norms(a):
                squares = work.tile([P, PACK, M_ALL], BF16, name="squares")
                for t in range(PACK):
                    nc.scalar.activation(
                        out=squares[:, t, :], in_=z_sb[a][:, t, :], func=ACT.Square,
                        accum_out=sum_sq[:, a, t : t + 1],
                    )
                nc.scalar.activation(out=t_out[:, a, :], in_=sum_sq[:, a, :], func=ACT.Sqrt, bias=1.0)

            def inverses(a):
                nc.vector.reciprocal(out=inv_t_out[:, a, :], in_=t_out[:, a, :])

            def slopes(a):
                nc.vector.tensor_tensor(out=slope[:, a, :], in0=g_tokens(a)[:, :, 0], in1=inv_t_out[:, a, :], op=ALU.mult)

            def rows(a):
                dz_rows[a] = work.tile([P, PACK, M_ALL], BF16, name="dz_rows")
                for t in range(PACK):
                    nc.vector.scalar_tensor_tensor(
                        out=dz_rows[a][:, t, :], in0=z_sb[a][:, t, :], scalar=slope[:, a, t : t + 1],
                        in1=g_tokens(a)[:, t, 1:G_IN], op0=ALU.mult, op1=ALU.add,
                    )

            def regroup_dz(a):
                dz_grouped[a] = work.tile([P, M_ALL, PACK], BF16, align_bytes=64, name="dz_grouped")
                if a < PASSES - 1:
                    src, dst = regrouped(dz_rows[a][:], dz_grouped[a][:])
                    nc.vector.tensor_copy(out=dst, in_=src)
                else:
                    src, dst = regrouped(dz_rows[a][:, :, 0:M_HALF], dz_grouped[a][:, 0:M_HALF, :])
                    nc.vector.tensor_copy(out=dst, in_=src)
                    src, dst = regrouped(dz_rows[a][:, :, M_HALF:M_ALL], dz_grouped[a][:, M_HALF:M_ALL, :])
                    nc.scalar.copy(out=dst, in_=src)

            def quantise_dz(a, half):
                cols = slice(half * M_HALF, (half + 1) * M_HALF)
                nc.vector.quantize_mx(
                    out=dz_codes[:, a, cols].bitcast(E5M2_X4),
                    scales=dz_scales[:, a, cols],
                    in_=dz_grouped[a][:, cols, :].rearrange("p m t -> p (m t)"),
                )

            def first_passes(a):
                for m in range(M_TILES):
                    for tap in FIRST_TAPS:
                        multiply(first_acc[(tap, m)], tap, m, a, a == 0, False)

            with tc.manual_schedule(engines={mybir.EngineType.DVE, mybir.EngineType.Activation}):
                norms(0)
                regroup_x(1, 1, nc.scalar.copy)
                inverses(0)
                slopes(0)
                rows(0)
                regroup_dz(0)
                norms(1)
                regroup_x(2, 1, nc.scalar.copy)
                quantise_x(1, 1)
                for a in range(1, PASSES):
                    inverses(a)
                    quantise_dz(a - 1, 0)
                    slopes(a)
                    quantise_dz(a - 1, 1)
                    rows(a)
                    quantise_x(a + 1, 1)
                    first_passes(a - 1)
                    regroup_dz(a)
                    if a + 1 < PASSES:
                        norms(a + 1)
                        regroup_x(a + 2, 1, nc.scalar.copy)
                quantise_dz(PASSES - 1, 0)
                quantise_dz(PASSES - 1, 1)

        def make_t_cat():
            time_sq = small.tile([P, ROW_TILES, SLOTS], F32, name="time_sq")
            nc.vector.tensor_tensor(out=time_sq[:], in0=x_win[:, :, :, 0], in1=x_win[:, :, :, 0], op=ALU.mult)
            pair_q = small.tile([P, ROW_TILES, PACK], F32, name="pair_q")
            nc.vector.tensor_tensor(out=pair_q[:], in0=time_sq[:, :, 0:PACK], in1=time_sq[:, :, 1 : 1 + PACK], op=ALU.add)
            sum_q = small.tile([P, ROW_TILES, PACK], F32, name="sum_q")
            nc.vector.tensor_tensor(out=sum_q[:], in0=pair_q[:], in1=time_sq[:, :, 2 : 2 + PACK], op=ALU.add)
            pair_r = small.tile([P, PASSES, PACK], F32, name="pair_r")
            nc.vector.tensor_tensor(out=pair_r[:], in0=sum_q[:, 0:PASSES, :], in1=sum_q[:, 1 : 1 + PASSES, :], op=ALU.add)
            sum_taps = small.tile([P, PASSES, PACK], F32, name="sum_taps")
            nc.vector.tensor_tensor(out=sum_taps[:], in0=pair_r[:], in1=sum_q[:, 2 : 2 + PASSES, :], op=ALU.add)
            nc.scalar.activation(out=t_cat[:], in_=sum_taps[:], func=ACT.Sqrt, bias=-8.0)

        later_tiles = [(BOTTOM, 1)]
        for i, j in LATER_TAPS:
            for a in range(PASSES):
                if (a + i, j) not in made and (a + i, j) not in later_tiles:
                    later_tiles.append((a + i, j))
        for k, tile in enumerate(later_tiles):
            if tile == (1, T_CAT_TAP[1]):
                make_t_cat()
            regroup_x(tile[0], tile[1], nc.vector.tensor_copy)
            if k > 0:
                quantise_x(later_tiles[k - 1][0], later_tiles[k - 1][1])
        quantise_x(later_tiles[-1][0], later_tiles[-1][1])

        rows_pool = stack.enter_context(tc.tile_pool(name="rows", bufs=1))
        out_rows = [rows_pool.tile([M_TILE, H_COLS], F32, name="out_rows%d" % m) for m in range(M_TILES)]
        stored = []

        def empty_and_store(acc, tap, m, cuts=()):
            n = 3 * tap[0] + tap[1]
            first = 1 + SPACE * n
            last = first + SPACE
            t_cat_n = 3 * T_CAT_TAP[0] + T_CAT_TAP[1]
            left_there = (n - 1 in stored) if n > 0 else (t_cat_n in stored)
            right_there = n + 1 in stored
            lo = first - first % STORE_ALIGN if left_there else first + (-first) % STORE_ALIGN
            hi = last + (-last) % STORE_ALIGN if right_there else last - last % STORE_ALIGN
            rows = slice(m * M_TILE, (m + 1) * M_TILE)
            for a, b in zip([first, *cuts], [*cuts, last]):
                nc.scalar.copy(out=out_rows[m][:, a:b], in_=acc[:, 1 + a - first : 1 + b - first])
                store = slice(lo if a == first else a, hi if b == last else b)
                nc.sync.dma_start(out=out[rows, store], in_=out_rows[m][:, store])
            if tap == T_CAT_TAP:
                nc.scalar.copy(out=out_rows[m][:, 0:1], in_=acc[:, 0:1])
                nc.sync.dma_start(out=out[rows, 0:STORE_ALIGN], in_=out_rows[m][:, 0:STORE_ALIGN])

        def open_tap():
            return [psum.tile([M_TILE, N_TILE], F32, name="acc%d" % m, tag="acc") for m in range(M_TILES)]

        def empty_tap(accs, tap):
            for m in range(M_TILES):
                empty_and_store(accs[m], tap, m)
            stored.append(3 * tap[0] + tap[1])

        def upper_tap(j, bank_by_bank):
            tap = (0, j)
            accs = open_tap()
            order = [1, 2, 3, 0]
            if bank_by_bank:
                for m in range(M_TILES):
                    for a in order:
                        multiply(accs[m], tap, m, a, a == order[0], a == order[-1])
                    middle = 1 + SPACE * (3 * tap[0] + tap[1]) + SPACE // 2
                    cuts = [middle - middle % STORE_ALIGN] if m == M_TILES - 1 else []
                    empty_and_store(accs[m], tap, m, cuts)
                stored.append(3 * tap[0] + tap[1])
            else:
                for a in order:
                    for m in range(M_TILES):
                        multiply(accs[m], tap, m, a, a == order[0], a == order[-1])
                empty_tap(accs, tap)

        def tap_pair(j):
            middle = open_tap()
            lower = open_tap()
            for u in range(1, ROW_TILES):
                if u - 1 < PASSES:
                    for m in range(M_TILES):
                        multiply(middle[m], (1, j), m, u - 1, u - 1 == 0, u - 1 == PASSES - 1)
                if u - 1 == PASSES - 1:
                    empty_tap(middle, (1, j))
                if u - 2 >= 0:
                    for m in range(M_TILES):
                        multiply(lower[m], (2, j), m, u - 2, u - 2 == 0, u - 2 == PASSES - 1)
            empty_tap(lower, (2, j))

        def close_first_tap(tap):
            accs = [first_acc[(tap, m)] for m in range(M_TILES)]
            for m in range(M_TILES):
                multiply(accs[m], tap, m, PASSES - 1, False, True)
            empty_tap(accs, tap)

        with tc.manual_schedule(engines={mybir.EngineType.PE}):
            close_first_tap((1, 1))
            upper = open_tap()
            for m in range(M_TILES):
                for a in range(1, PASSES):
                    multiply(upper[m], (0, 1), m, a, a == 1, False)
            close_first_tap((2, 1))
            for m in range(M_TILES):
                multiply(upper[m], (0, 1), m, 0, False, True)
            empty_tap(upper, (0, 1))
            tap_pair(0)
            upper_tap(0, False)
            tap_pair(2)
            upper_tap(2, True)
